import numpy as np
import ml_dtypes


def mxq(x, axis, fmt="e4m3"):
    dtype, down = {"e4m3": (ml_dtypes.float8_e4m3fn, 7), "e5m2": (ml_dtypes.float8_e5m2, 14)}[fmt]
    v = np.moveaxis(np.asarray(x, np.float32).astype(ml_dtypes.bfloat16).astype(np.float64), axis, -1)
    blocks = v.reshape(v.shape[:-1] + (-1, 32))
    amax = np.abs(blocks).max(-1, keepdims=True)
    byte = np.maximum(np.where(amax > 0, np.frexp(amax)[1] - 1 + 127, 0) - down, 1)
    scale = np.exp2(byte - 127.0)
    codes = (blocks / scale).astype(np.float32).astype(dtype).astype(np.float64)
    return np.moveaxis((codes * scale).reshape(v.shape), -1, axis)


WIDE = False


def mx_kscale(k):
    if not WIDE:
        return np.ones(k)
    levels = np.array([10, -10, 5, -5, 0])
    a = np.random.permutation(np.resize(levels, k // 512 * 4)).reshape(k // 512, 4)
    idx = np.arange(k)
    return np.exp2(a[idx // 512, idx % 128 // 32])


BF16 = ml_dtypes.bfloat16


def bf(x):
    return np.asarray(x, np.float32).astype(BF16)


def f64(x):
    return np.asarray(x).astype(np.float64)


B, CIN, CMID, C4, C8, COUT, T, H, W = 4, 512, 1024, 256, 128, 128, 8, 16, 16
S = T * H * W


def setup_inputs():
    s = mx_kscale(CMID)
    h_add = np.maximum(np.random.standard_normal((B, CMID, S)) * np.sqrt(2.0), 0.0)
    h_occ = np.maximum(np.random.standard_normal((B, C8, S)) * np.sqrt(2.0), 0.0)
    return {"h_add": bf(h_add * s[None, :, None]),
            "w_add2": bf(np.random.standard_normal((CIN, CMID)) * np.sqrt(2.0 / CMID) / s[None, :]),
            "b_add2": bf(np.random.standard_normal(CIN) * 0.3),
            "h_occ": bf(h_occ),
            "w_occ3": bf(np.random.standard_normal((COUT, C8)) / np.sqrt(C8))}


def reference(h_add, w_add2, b_add2, h_occ, w_occ3):
    feat = (mxq(f64(w_add2), 1, "e4m3") @ mxq(f64(h_add), 1, "e4m3")) + f64(b_add2)[None, :, None]
    occ = np.abs(f64(w_occ3) @ f64(h_occ))
    return (mxq(occ, 2, "e4m3") @ mxq(feat, 2, "e4m3").transpose(0, 2, 1)) / S

@@ -1,0 +1,285 @@
+from contextlib import ExitStack
+
+import concourse.bass as bass
+import concourse.mybir as mybir
+import concourse.tile as tile
+from concourse.masks import make_identity
+
+F32 = mybir.dt.float32
+BF16 = mybir.dt.bfloat16
+U32 = mybir.dt.uint32
+U8 = mybir.dt.uint8
+FP8X4 = mybir.dt.float8_e4m3fn_x4
+ADD = mybir.AluOpType.add
+MULT = mybir.AluOpType.mult
+ACT = mybir.ActivationFunctionType
+
+P = 128
+B, CIN, CMID, C8, COUT, S = 4, 512, 1024, 128, 128, 2048
+KP = CMID // 512
+RV = 512
+NG = S // RV
+NR = B * NG
+NCT = CIN // P
+
+FLOPS = 2 * B * S * (CIN * CMID + COUT * C8 + COUT * CIN)
+
+MANUAL = True
+LS = 4
+LV = 3
+LO = 3
+VSHARE = 96
+VFULL = ((0, 0), (0, 1))
+GSHARE = 0
+QORDER = "HOF"
+NBG = 3
+NPS = 6
+
+
+def tile_occurrencepool_pa_t_kernel(tc, h_add, w_add2, b_add2, h_occ, w_occ3, out):
+    nc = tc.nc
+    with ExitStack() as ctx:
+        const = ctx.enter_context(tc.tile_pool(name="const", bufs=1))
+        rawp = ctx.enter_context(tc.tile_pool(name="rawp", bufs=4))
+        grpp = ctx.enter_context(tc.tile_pool(name="grpp", bufs=NBG))
+        hcp = ctx.enter_context(tc.tile_pool(name="hcp", bufs=2))
+        fp = ctx.enter_context(tc.tile_pool(name="fp", bufs=2))
+        op = ctx.enter_context(tc.tile_pool(name="op", bufs=3))
+        outp = ctx.enter_context(tc.tile_pool(name="outp", bufs=2))
+        psum = ctx.enter_context(tc.psum_pool(name="psum", bufs=NPS))
+        accp = ctx.enter_context(tc.psum_pool(name="accp", bufs=2))
+        if MANUAL:
+            ctx.enter_context(tc.manual_schedule())
+
+        raw = {}
+
+        def load_h(b, kp, v0, nv, pool, tag):
+            t = pool.tile([P, 4 * nv], BF16, name="raw", tag=tag)
+            view = t[:].rearrange("p (t v) -> p t v", t=4)
+            rows = h_add[b, 512 * kp : 512 * kp + 512, v0 : v0 + nv]
+            nc.sync.dma_start(out=view, in_=rows.rearrange("(p t) v -> p t v", t=4))
+            for g in range(v0 // RV, (v0 + nv) // RV):
+                raw[(b, kp, g)] = view[:, :, g * RV - v0 : g * RV - v0 + RV]
+
+        hocc = {}
+
+        def load_hocc(b):
+            t = const.tile([P, S], BF16, name="hocc", tag="hocc%d" % b)
+            nc.sync.dma_start(out=t[:], in_=h_occ[b])
+            hocc[b] = t
+
+        ones = const.tile([P, P], BF16, name="ones")
+        nc.vector.memset(ones[:], 1.0)
+        brow = const.tile([P, CIN], BF16, name="brow")
+        nc.vector.memset(brow[:], 0.0)
+        wo_raw = const.tile([P, C8], BF16, name="wo_raw")
+        nc.scalar.dma_start(out=wo_raw[:], in_=w_occ3)
+        nc.scalar.dma_start(out=brow[0:1, :], in_=b_add2.unsqueeze(0))
+
+        w_raw = const.tile([P, NCT * CMID], BF16, name="w_raw")
+        nc.sync.dma_start(
+            out=w_raw[:].rearrange("p (a k) -> p a k", a=NCT),
+            in_=w_add2.rearrange("(a p) k -> p a k", p=P),
+        )
+        load_h(0, 0, 0, 512, const, "r000")
+        load_h(0, 1, 0, 512, const, "r010")
+        load_h(0, 0, 512, 512, const, "r001")
+        load_h(0, 1, 512, 512, const, "r011")
+        load_hocc(0)
+        load_h(0, 0, 1024, 1024, const, "r00h")
+        load_h(0, 1, 1024, 1024, const, "r01h")
+        load_h(1, 0, 0, S, rawp, "raw")
+        load_h(1, 1, 0, S, rawp, "raw")
+        load_hocc(1)
+        load_h(2, 0, 0, S, rawp, "raw")
+        load_h(2, 1, 0, S, rawp, "raw")
+        load_hocc(2)
+        load_hocc(3)
+
+        ident_f = const.tile([P, P], F32, name="ident_f")
+        make_identity(nc, ident_f[:])
+        ident_b = const.tile([P, P], BF16, name="ident_b")
+        make_identity(nc, ident_b[:])
+        scr = const.tile([P, 1], F32, name="scr")
+        nc.scalar.activation(out=scr[:], in_=ones[:, 0:1], func=ACT.Abs)
+
+        wo_ps = psum.tile([P, P], BF16, name="wo_ps", tag="bank")
+        nc.tensor.transpose(out=wo_ps[:], in_=wo_raw[:], identity=ident_b[:])
+        woT = const.tile([P, COUT], BF16, name="woT")
+        nc.scalar.copy(out=woT[:], in_=wo_ps[:])
+
+        b_ps = psum.tile([P, CIN], F32, name="b_ps", tag="bank")
+        nc.tensor.matmul(out=b_ps[:], lhsT=ones[:], rhs=brow[:], start=True, stop=True)
+        bias = const.tile([P, CIN], F32, name="bias")
+        nc.scalar.copy(out=bias[:], in_=b_ps[:])
+
+        wf = w_raw[:].bitcast(F32)
+        wgrp = const.tile([P, KP * CIN * 4], BF16, name="wgrp", align_bytes=64)
+        wgf = wgrp[:].bitcast(F32).rearrange("p (k c u) -> p k c u", k=KP, c=CIN, u=2)
+        wc = const.tile([P, KP * CIN], U32, name="wc", align_bytes=64)
+        ws = const.tile([P, KP * CIN], U8, name="ws", align_bytes=64)
+        for kp in range(KP):
+            for cp in range(NCT // 2):
+                w_ps = psum.tile([P, 2, 2 * P], F32, name="w_ps", tag="bank")
+                for u in range(2):
+                    for h in range(2):
+                        w0 = (2 * cp + h) * 512 + 256 * kp
+                        nc.tensor.transpose(
+                            out=w_ps[:, u, h * P : (h + 1) * P],
+                            in_=wf[:, w0 + u : w0 + 256 : 2],
+                            identity=ident_f[:],
+                        )
+                nc.scalar.copy(
+                    out=wgf[:, kp, 2 * cp * P : (2 * cp + 2) * P, :],
+                    in_=w_ps[:].rearrange("p u c -> p c u"),
+                )
+
+        def quantise_w():
+            for kp in range(KP):
+                nc.vector.quantize_mx(
+                    out=wc[:, kp * CIN : (kp + 1) * CIN].bitcast(FP8X4),
+                    scales=ws[:, kp * CIN : (kp + 1) * CIN],
+                    in_=wgrp[:, kp * CIN * 4 : (kp + 1) * CIN * 4],
+                )
+
+        grp, hc, hs, banks, fg, fc, fs = {}, {}, {}, {}, {}, {}, {}
+        obank, og, oc, os_, acc = {}, {}, {}, {}, {}
+
+        def segments(r, kp):
+            if (r, kp) in VFULL:
+                return [("v", 0, RV)]
+            if kp == 0:
+                return [("s", 0, RV)]
+            segs = [("s", 0, RV - VSHARE - GSHARE)]
+            if GSHARE:
+                segs.append(("g", RV - VSHARE - GSHARE, RV - VSHARE))
+            if VSHARE:
+                segs.append(("v", RV - VSHARE, RV))
+            return segs
+
+        def regroup(r, engines):
+            b, g = divmod(r, NG)
+            for kp in range(KP):
+                for eng, v0, v1 in segments(r, kp):
+                    if eng not in engines:
+                        continue
+                    if r not in grp:
+                        grp[r] = grpp.tile([P, KP * RV * 4], BF16, name="grp", align_bytes=64)
+                    dst = grp[r][:].rearrange("p (k v t) -> p k v t", k=KP, v=RV, t=4)
+                    dst = dst[:, kp, v0:v1, :].rearrange("p (c i) t -> p c t i", i=4)
+                    src = raw[(b, kp, g)][:, :, v0:v1].rearrange("p t (c i) -> p c t i", i=4)
+                    if eng == "v":
+                        nc.vector.tensor_copy(out=dst, in_=src)
+                    elif eng == "s":
+                        nc.scalar.copy(out=dst, in_=src)
+                    else:
+                        nc.gpsimd.tensor_scalar(out=dst, in0=src, scalar1=1.0, scalar2=0.0, op0=MULT, op1=ADD)
+
+        def quantise_h(r):
+            hc[r] = hcp.tile([P, KP * RV], U32, name="hc", align_bytes=64)
+            hs[r] = hcp.tile([P, KP * RV], U8, name="hs", align_bytes=64)
+            nc.vector.quantize_mx(out=hc[r][:].bitcast(FP8X4), scales=hs[r][:], in_=grp[r][:])
+
+        def stage1(r, ct):
+            ps = psum.tile([P, 4, P], F32, name="ps", tag="bank")
+            banks[(r, ct)] = ps
+            for j in range(4):
+                for kp in range(KP):
+                    hcol = slice(kp * RV + j * P, kp * RV + (j + 1) * P)
+                    wcol = slice(kp * CIN + ct * P, kp * CIN + (ct + 1) * P)
+                    nc.tensor.matmul_mx(
+                        out=ps[:, j, :],
+                        lhsT=hc[r][:, hcol].bitcast(FP8X4),
+                        lhsT_scale=hs[r][:, hcol],
+                        rhs=wc[:, wcol].bitcast(FP8X4),
+                        rhs_scale=ws[:, wcol],
+                        start=(kp == 0),
+                        stop=(kp == KP - 1),
+                    )
+
+        def evacuate(r, ct):
+            if ct == 0:
+                fg[r] = fp.tile([P, CIN * 4], BF16, name="fg", align_bytes=64)
+            dst = fg[r][:].rearrange("p (c j) -> p c j", j=4)[:, ct * P : (ct + 1) * P, :]
+            nc.vector.tensor_tensor(
+                out=dst,
+                in0=banks[(r, ct)][:].rearrange("p j c -> p c j"),
+                in1=bias[:, ct * P : (ct + 1) * P].unsqueeze(2).to_broadcast([P, P, 4]),
+                op=ADD,
+            )
+
+        def quantise_f(r):
+            fc[r] = fp.tile([P, CIN], U32, name="fc", align_bytes=64)
+            fs[r] = fp.tile([P, CIN], U8, name="fs", align_bytes=64)
+            nc.vector.quantize_mx(out=fc[r][:].bitcast(FP8X4), scales=fs[r][:], in_=fg[r][:])
+
+        def occurrence(r):
+            b, g = divmod(r, NG)
+            ps = psum.tile([P, 4, P], F32, name="ops", tag="bank")
+            for j in range(4):
+                v0 = g * RV + j * P
+                nc.tensor.matmul(out=ps[:, j, :], lhsT=hocc[b][:, v0 : v0 + P], rhs=woT[:], start=True, stop=True)
+            og[r] = op.tile([P, COUT * 4], BF16, name="og", align_bytes=64)
+            nc.scalar.activation(
+                out=og[r][:].rearrange("p (o j) -> p o j", j=4),
+                in_=ps[:].rearrange("p j o -> p o j"),
+                func=ACT.Abs,
+            )
+
+        def quantise_o(r):
+            oc[r] = op.tile([P, COUT], U32, name="oc", align_bytes=64)
+            os_[r] = op.tile([P, COUT], U8, name="os", align_bytes=64)
+            nc.vector.quantize_mx(out=oc[r][:].bitcast(FP8X4), scales=os_[r][:], in_=og[r][:])
+
+        def stage2(r):
+            b, g = divmod(r, NG)
+            if g == 0:
+                acc[b] = accp.tile([P, CIN], F32, name="acc")
+            nc.tensor.matmul_mx(
+                out=acc[b][:],
+                lhsT=oc[r][:].bitcast(FP8X4),
+                lhsT_scale=os_[r][:],
+                rhs=fc[r][:].bitcast(FP8X4),
+                rhs_scale=fs[r][:],
+                start=(g == 0),
+                stop=(g == NG - 1),
+            )
+
+        def finish(b):
+            ob = outp.tile([P, CIN], F32, name="ob")
+            nc.scalar.mul(out=ob[:], in_=acc[b][:], mul=1.0 / S)
+            nc.sync.dma_start(out=out[b], in_=ob[:])
+
+        def live(r):
+            return 0 <= r < NR
+
+        for i in range(-LS, NR + 1):
+            if live(i + LS):
+                regroup(i + LS, "sg")
+            if live(i + 1):
+                stage1(i + 1, 0)
+            if live(i - 1):
+                stage2(i - 1)
+            for ct in range(NCT):
+                if live(i):
+                    evacuate(i, ct)
+                if ct + 1 < NCT and live(i + 1):
+                    stage1(i + 1, ct + 1)
+            if live(i + LO):
+                occurrence(i + LO)
+            for q in QORDER:
+                if q == "H" and live(i + 2):
+                    quantise_h(i + 2)
+                    if i + 2 == 0:
+                        quantise_w()
+                if q == "O" and live(i + 1):
+                    quantise_o(i + 1)
+                if q == "F" and live(i):
+                    quantise_f(i)
+            if live(i + LV):
+                regroup(i + LV, "v")
+            if i == 4:
+                load_h(3, 0, 0, S, rawp, "raw")
+                load_h(3, 1, 0, S, rawp, "raw")
+            if i >= NG and i % NG == 0:
+                finish(i // NG - 1)

@@ -1,8 +1,6 @@
 from contextlib import ExitStack
 
-import concourse.bass as bass
 import concourse.mybir as mybir
-import concourse.tile as tile
 from concourse.masks import make_identity
 
 F32 = mybir.dt.float32
@@ -28,19 +26,22 @@ MANUAL = True
 LS = 4
 LV = 3
 LO = 3
-VSHARE = 96
-VFULL = ((0, 0), (0, 1))
+VSHARE = 128
+VLATE = 128
+LATE = 13
+WHOLE = {(0, 0): "s", (0, 1): "v", (1, 0): "v", (1, 1): "v"}
 GSHARE = 0
+GFROM = 3
 QORDER = "HOF"
 NBG = 3
 NPS = 6
+SPLIT_LAST = True
 
 
 def tile_occurrencepool_pa_t_kernel(tc, h_add, w_add2, b_add2, h_occ, w_occ3, out):
     nc = tc.nc
     with ExitStack() as ctx:
         const = ctx.enter_context(tc.tile_pool(name="const", bufs=1))
-        rawp = ctx.enter_context(tc.tile_pool(name="rawp", bufs=4))
         grpp = ctx.enter_context(tc.tile_pool(name="grpp", bufs=NBG))
         hcp = ctx.enter_context(tc.tile_pool(name="hcp", bufs=2))
         fp = ctx.enter_context(tc.tile_pool(name="fp", bufs=2))
@@ -53,8 +54,8 @@ def tile_occurrencepool_pa_t_kernel(tc, h_add, w_add2, b_add2, h_occ, w_occ3, ou
 
         raw = {}
 
-        def load_h(b, kp, v0, nv, pool, tag):
-            t = pool.tile([P, 4 * nv], BF16, name="raw", tag=tag)
+        def load_h(b, kp, v0, nv):
+            t = const.tile([P, 4 * nv], BF16, name="raw", tag="raw%d_%d_%d" % (b, kp, v0))
             view = t[:].rearrange("p (t v) -> p t v", t=4)
             rows = h_add[b, 512 * kp : 512 * kp + 512, v0 : v0 + nv]
             nc.sync.dma_start(out=view, in_=rows.rearrange("(p t) v -> p t v", t=4))
@@ -73,96 +74,56 @@ def tile_occurrencepool_pa_t_kernel(tc, h_add, w_add2, b_add2, h_occ, w_occ3, ou
         brow = const.tile([P, CIN], BF16, name="brow")
         nc.vector.memset(brow[:], 0.0)
         wo_raw = const.tile([P, C8], BF16, name="wo_raw")
-        nc.scalar.dma_start(out=wo_raw[:], in_=w_occ3)
-        nc.scalar.dma_start(out=brow[0:1, :], in_=b_add2.unsqueeze(0))
+        nc.sync.dma_start(out=wo_raw[:], in_=w_occ3)
+        nc.sync.dma_start(out=brow[0:1, :], in_=b_add2.unsqueeze(0))
 
         w_raw = const.tile([P, NCT * CMID], BF16, name="w_raw")
+        load_h(0, 0, 0, RV)
+        load_h(0, 1, 0, RV)
         nc.sync.dma_start(
             out=w_raw[:].rearrange("p (a k) -> p a k", a=NCT),
             in_=w_add2.rearrange("(a p) k -> p a k", p=P),
         )
-        load_h(0, 0, 0, 512, const, "r000")
-        load_h(0, 1, 0, 512, const, "r010")
-        load_h(0, 0, 512, 512, const, "r001")
-        load_h(0, 1, 512, 512, const, "r011")
+        load_h(0, 0, RV, RV)
+        load_h(0, 1, RV, RV)
         load_hocc(0)
-        load_h(0, 0, 1024, 1024, const, "r00h")
-        load_h(0, 1, 1024, 1024, const, "r01h")
-        load_h(1, 0, 0, S, rawp, "raw")
-        load_h(1, 1, 0, S, rawp, "raw")
+        for g in (2, 3):
+            load_h(0, 0, g * RV, RV)
+            load_h(0, 1, g * RV, RV)
+        for h in (0, 1):
+            load_h(1, 0, h * 2 * RV, 2 * RV)
+            load_h(1, 1, h * 2 * RV, 2 * RV)
         load_hocc(1)
-        load_h(2, 0, 0, S, rawp, "raw")
-        load_h(2, 1, 0, S, rawp, "raw")
-        load_hocc(2)
-        load_hocc(3)
-
-        ident_f = const.tile([P, P], F32, name="ident_f")
-        make_identity(nc, ident_f[:])
-        ident_b = const.tile([P, P], BF16, name="ident_b")
-        make_identity(nc, ident_b[:])
-        scr = const.tile([P, 1], F32, name="scr")
-        nc.scalar.activation(out=scr[:], in_=ones[:, 0:1], func=ACT.Abs)
-
-        wo_ps = psum.tile([P, P], BF16, name="wo_ps", tag="bank")
-        nc.tensor.transpose(out=wo_ps[:], in_=wo_raw[:], identity=ident_b[:])
-        woT = const.tile([P, COUT], BF16, name="woT")
-        nc.scalar.copy(out=woT[:], in_=wo_ps[:])
-
-        b_ps = psum.tile([P, CIN], F32, name="b_ps", tag="bank")
-        nc.tensor.matmul(out=b_ps[:], lhsT=ones[:], rhs=brow[:], start=True, stop=True)
-        bias = const.tile([P, CIN], F32, name="bias")
-        nc.scalar.copy(out=bias[:], in_=b_ps[:])
-
-        wf = w_raw[:].bitcast(F32)
-        wgrp = const.tile([P, KP * CIN * 4], BF16, name="wgrp", align_bytes=64)
-        wgf = wgrp[:].bitcast(F32).rearrange("p (k c u) -> p k c u", k=KP, c=CIN, u=2)
-        wc = const.tile([P, KP * CIN], U32, name="wc", align_bytes=64)
-        ws = const.tile([P, KP * CIN], U8, name="ws", align_bytes=64)
-        for kp in range(KP):
-            for cp in range(NCT // 2):
-                w_ps = psum.tile([P, 2, 2 * P], F32, name="w_ps", tag="bank")
-                for u in range(2):
-                    for h in range(2):
-                        w0 = (2 * cp + h) * 512 + 256 * kp
-                        nc.tensor.transpose(
-                            out=w_ps[:, u, h * P : (h + 1) * P],
-                            in_=wf[:, w0 + u : w0 + 256 : 2],
-                            identity=ident_f[:],
-                        )
-                nc.scalar.copy(
-                    out=wgf[:, kp, 2 * cp * P : (2 * cp + 2) * P, :],
-                    in_=w_ps[:].rearrange("p u c -> p c u"),
-                )
-
-        def quantise_w():
-            for kp in range(KP):
-                nc.vector.quantize_mx(
-                    out=wc[:, kp * CIN : (kp + 1) * CIN].bitcast(FP8X4),
-                    scales=ws[:, kp * CIN : (kp + 1) * CIN],
-                    in_=wgrp[:, kp * CIN * 4 : (kp + 1) * CIN * 4],
-                )
+        for b in (2, 3):
+            load_h(b, 0, 0, S)
+            load_h(b, 1, 0, S)
+            load_hocc(b)
 
         grp, hc, hs, banks, fg, fc, fs = {}, {}, {}, {}, {}, {}, {}
-        obank, og, oc, os_, acc = {}, {}, {}, {}, {}
+        og, oc, os_, acc = {}, {}, {}, {}
+        emitted = set()
 
         def segments(r, kp):
-            if (r, kp) in VFULL:
-                return [("v", 0, RV)]
+            if (r, kp) in WHOLE:
+                return [(WHOLE[(r, kp)], 0, RV)]
             if kp == 0:
                 return [("s", 0, RV)]
-            segs = [("s", 0, RV - VSHARE - GSHARE)]
-            if GSHARE:
-                segs.append(("g", RV - VSHARE - GSHARE, RV - VSHARE))
-            if VSHARE:
-                segs.append(("v", RV - VSHARE, RV))
+            vs = VLATE if r >= LATE else VSHARE
+            gs = GSHARE if r >= GFROM else 0
+            segs = [("s", 0, RV - vs - gs)]
+            if gs:
+                segs.append(("g", RV - vs - gs, RV - vs))
+            if vs:
+                segs.append(("v", RV - vs, RV))
             return segs
 
         def regroup(r, engines):
             b, g = divmod(r, NG)
             for kp in range(KP):
                 for eng, v0, v1 in segments(r, kp):
-                    if eng not in engines:
+                    if eng not in engines or (r, kp, v0) in emitted:
                         continue
+                    emitted.add((r, kp, v0))
                     if r not in grp:
                         grp[r] = grpp.tile([P, KP * RV * 4], BF16, name="grp", align_bytes=64)
                     dst = grp[r][:].rearrange("p (k v t) -> p k v t", k=KP, v=RV, t=4)
@@ -176,6 +137,9 @@ def tile_occurrencepool_pa_t_kernel(tc, h_add, w_add2, b_add2, h_occ, w_occ3, ou
                         nc.gpsimd.tensor_scalar(out=dst, in0=src, scalar1=1.0, scalar2=0.0, op0=MULT, op1=ADD)
 
         def quantise_h(r):
+            if ("qh", r) in emitted:
+                return
+            emitted.add(("qh", r))
             hc[r] = hcp.tile([P, KP * RV], U32, name="hc", align_bytes=64)
             hs[r] = hcp.tile([P, KP * RV], U8, name="hs", align_bytes=64)
             nc.vector.quantize_mx(out=hc[r][:].bitcast(FP8X4), scales=hs[r][:], in_=grp[r][:])
@@ -208,12 +172,18 @@ def tile_occurrencepool_pa_t_kernel(tc, h_add, w_add2, b_add2, h_occ, w_occ3, ou
                 op=ADD,
             )
 
-        def quantise_f(r):
-            fc[r] = fp.tile([P, CIN], U32, name="fc", align_bytes=64)
-            fs[r] = fp.tile([P, CIN], U8, name="fs", align_bytes=64)
-            nc.vector.quantize_mx(out=fc[r][:].bitcast(FP8X4), scales=fs[r][:], in_=fg[r][:])
+        def quantise_f(r, c0, c1):
+            if c0 == 0:
+                fc[r] = fp.tile([P, CIN], U32, name="fc", align_bytes=64)
+                fs[r] = fp.tile([P, CIN], U8, name="fs", align_bytes=64)
+            nc.vector.quantize_mx(
+                out=fc[r][:, c0:c1].bitcast(FP8X4), scales=fs[r][:, c0:c1], in_=fg[r][:, 4 * c0 : 4 * c1]
+            )
 
         def occurrence(r):
+            if ("occ", r) in emitted:
+                return
+            emitted.add(("occ", r))
             b, g = divmod(r, NG)
             ps = psum.tile([P, 4, P], F32, name="ops", tag="bank")
             for j in range(4):
@@ -227,59 +197,120 @@ def tile_occurrencepool_pa_t_kernel(tc, h_add, w_add2, b_add2, h_occ, w_occ3, ou
             )
 
         def quantise_o(r):
+            if ("qo", r) in emitted:
+                return
+            emitted.add(("qo", r))
             oc[r] = op.tile([P, COUT], U32, name="oc", align_bytes=64)
             os_[r] = op.tile([P, COUT], U8, name="os", align_bytes=64)
             nc.vector.quantize_mx(out=oc[r][:].bitcast(FP8X4), scales=os_[r][:], in_=og[r][:])
 
-        def stage2(r):
+        def halves(b):
+            if SPLIT_LAST and b == B - 1:
+                return [(0, CIN // 2), (CIN // 2, CIN)]
+            return [(0, CIN)]
+
+        def stage2(r, c0, c1):
             b, g = divmod(r, NG)
             if g == 0:
-                acc[b] = accp.tile([P, CIN], F32, name="acc")
+                acc[(b, c0)] = accp.tile([P, c1 - c0], F32, name="acc")
             nc.tensor.matmul_mx(
-                out=acc[b][:],
+                out=acc[(b, c0)][:],
                 lhsT=oc[r][:].bitcast(FP8X4),
                 lhsT_scale=os_[r][:],
-                rhs=fc[r][:].bitcast(FP8X4),
-                rhs_scale=fs[r][:],
+                rhs=fc[r][:, c0:c1].bitcast(FP8X4),
+                rhs_scale=fs[r][:, c0:c1],
                 start=(g == 0),
                 stop=(g == NG - 1),
             )
 
-        def finish(b):
-            ob = outp.tile([P, CIN], F32, name="ob")
-            nc.scalar.mul(out=ob[:], in_=acc[b][:], mul=1.0 / S)
-            nc.sync.dma_start(out=out[b], in_=ob[:])
+        def finish(b, c0, c1):
+            ob = outp.tile([P, c1 - c0], F32, name="ob")
+            nc.scalar.mul(out=ob[:], in_=acc[(b, c0)][:], mul=1.0 / S)
+            nc.sync.dma_start(out=out[b, :, c0:c1], in_=ob[:])
+
+        ident_f = const.tile([P, P], F32, name="ident_f")
+        make_identity(nc, ident_f[:])
+        ident_b = const.tile([P, P], BF16, name="ident_b")
+        make_identity(nc, ident_b[:])
+        scr = const.tile([P, 1], F32, name="scr")
+        nc.scalar.activation(out=scr[:], in_=ones[:, 0:1], func=ACT.Abs)
+
+        wo_ps = psum.tile([P, P], BF16, name="wo_ps", tag="bank")
+        nc.tensor.transpose(out=wo_ps[:], in_=wo_raw[:], identity=ident_b[:])
+        woT = const.tile([P, COUT], BF16, name="woT")
+        nc.scalar.copy(out=woT[:], in_=wo_ps[:])
+
+        b_ps = psum.tile([P, CIN], F32, name="b_ps", tag="bank")
+        nc.tensor.matmul(out=b_ps[:], lhsT=ones[:], rhs=brow[:], start=True, stop=True)
+        bias = const.tile([P, CIN], F32, name="bias")
+        nc.scalar.copy(out=bias[:], in_=b_ps[:])
+
+        regroup(0, "sv")
+        quantise_h(0)
+
+        wf = w_raw[:].bitcast(F32)
+        wgrp = const.tile([P, KP * CIN * 4], BF16, name="wgrp", align_bytes=64)
+        wgf = wgrp[:].bitcast(F32).rearrange("p (k c u) -> p k c u", k=KP, c=CIN, u=2)
+        wc = const.tile([P, KP * CIN], U32, name="wc", align_bytes=64)
+        ws = const.tile([P, KP * CIN], U8, name="ws", align_bytes=64)
+        for kp in range(KP):
+            for cp in range(NCT // 2):
+                w_ps = psum.tile([P, 2, 2 * P], F32, name="w_ps", tag="bank")
+                for u in range(2):
+                    for h in range(2):
+                        w0 = (2 * cp + h) * 512 + 256 * kp
+                        nc.tensor.transpose(
+                            out=w_ps[:, u, h * P : (h + 1) * P],
+                            in_=wf[:, w0 + u : w0 + 256 : 2],
+                            identity=ident_f[:],
+                        )
+                nc.scalar.copy(
+                    out=wgf[:, kp, 2 * cp * P : (2 * cp + 2) * P, :],
+                    in_=w_ps[:].rearrange("p u c -> p c u"),
+                )
+        regroup(1, "sv")
+        for kp in range(KP):
+            nc.vector.quantize_mx(
+                out=wc[:, kp * CIN : (kp + 1) * CIN].bitcast(FP8X4),
+                scales=ws[:, kp * CIN : (kp + 1) * CIN],
+                in_=wgrp[:, kp * CIN * 4 : (kp + 1) * CIN * 4],
+            )
+        quantise_h(1)
+        occurrence(0)
+        quantise_o(0)
 
         def live(r):
             return 0 <= r < NR
 
+        last = NR - 1
         for i in range(-LS, NR + 1):
             if live(i + LS):
                 regroup(i + LS, "sg")
             if live(i + 1):
                 stage1(i + 1, 0)
-            if live(i - 1):
-                stage2(i - 1)
+            if live(i - 1) and not (SPLIT_LAST and i - 1 == last):
+                for c0, c1 in halves((i - 1) // NG):
+                    stage2(i - 1, c0, c1)
             for ct in range(NCT):
                 if live(i):
                     evacuate(i, ct)
                 if ct + 1 < NCT and live(i + 1):
                     stage1(i + 1, ct + 1)
+                if SPLIT_LAST and i == last and ct % 2 == 1:
+                    c0, c1 = halves(B - 1)[ct // 2]
+                    quantise_f(i, c0, c1)
+                    stage2(i, c0, c1)
+                    finish(B - 1, c0, c1)
             if live(i + LO):
                 occurrence(i + LO)
             for q in QORDER:
                 if q == "H" and live(i + 2):
                     quantise_h(i + 2)
-                    if i + 2 == 0:
-                        quantise_w()
                 if q == "O" and live(i + 1):
                     quantise_o(i + 1)
-                if q == "F" and live(i):
-                    quantise_f(i)
+                if q == "F" and live(i) and not (SPLIT_LAST and i == last):
+                    quantise_f(i, 0, CIN)
             if live(i + LV):
                 regroup(i + LV, "v")
-            if i == 4:
-                load_h(3, 0, 0, S, rawp, "raw")
-                load_h(3, 1, 0, S, rawp, "raw")
-            if i >= NG and i % NG == 0:
-                finish(i // NG - 1)
+            if i >= NG and i % NG == 0 and not (SPLIT_LAST and i == NR):
+                finish(i // NG - 1, 0, CIN)

@@ -27,12 +27,12 @@ LS = 4
 LV = 3
 LO = 3
 VSHARE = 128
-VLATE = 128
-LATE = 13
+VLATE = 0
+LATE = 99
 WHOLE = {(0, 0): "s", (0, 1): "v", (1, 0): "v", (1, 1): "v"}
-GSHARE = 0
-GFROM = 3
-QORDER = "HOF"
+GSHARE = 192
+GFROM = 4
+QORDER = "OFH"
 NBG = 3
 NPS = 6
 SPLIT_LAST = True
@@ -95,8 +95,9 @@ def tile_occurrencepool_pa_t_kernel(tc, h_add, w_add2, b_add2, h_occ, w_occ3, ou
             load_h(1, 1, h * 2 * RV, 2 * RV)
         load_hocc(1)
         for b in (2, 3):
-            load_h(b, 0, 0, S)
-            load_h(b, 1, 0, S)
+            for h in (0, 1):
+                load_h(b, 0, h * 2 * RV, 2 * RV)
+                load_h(b, 1, h * 2 * RV, 2 * RV)
             load_hocc(b)
 
         grp, hc, hs, banks, fg, fc, fs = {}, {}, {}, {}, {}, {}, {}
@@ -108,8 +109,8 @@ def tile_occurrencepool_pa_t_kernel(tc, h_add, w_add2, b_add2, h_occ, w_occ3, ou
                 return [(WHOLE[(r, kp)], 0, RV)]
             if kp == 0:
                 return [("s", 0, RV)]
-            vs = VLATE if r >= LATE else VSHARE
             gs = GSHARE if r >= GFROM else 0
+            vs = VLATE if r >= LATE else (0 if gs else VSHARE)
             segs = [("s", 0, RV - vs - gs)]
             if gs:
                 segs.append(("g", RV - vs - gs, RV - vs))
@@ -277,6 +278,7 @@ def tile_occurrencepool_pa_t_kernel(tc, h_add, w_add2, b_add2, h_occ, w_occ3, ou
             )
         quantise_h(1)
         occurrence(0)
+        occurrence(1)
         quantise_o(0)
 
         def live(r):

@@ -22,20 +22,16 @@ NCT = CIN // P
 
 FLOPS = 2 * B * S * (CIN * CMID + COUT * C8 + COUT * CIN)
 
-MANUAL = True
 LS = 4
 LV = 3
-LO = 3
+LO = 2
 VSHARE = 128
-VLATE = 0
-LATE = 99
-WHOLE = {(0, 0): "s", (0, 1): "v", (1, 0): "v", (1, 1): "v"}
+WHOLE = {(0, 0): "v", (0, 1): "v", (1, 0): "s", (1, 1): "v"}
 GSHARE = 192
-GFROM = 4
+GFROM = 2
 QORDER = "OFH"
 NBG = 3
 NPS = 6
-SPLIT_LAST = True
 
 
 def tile_occurrencepool_pa_t_kernel(tc, h_add, w_add2, b_add2, h_occ, w_occ3, out):
@@ -49,25 +45,30 @@ def tile_occurrencepool_pa_t_kernel(tc, h_add, w_add2, b_add2, h_occ, w_occ3, ou
         outp = ctx.enter_context(tc.tile_pool(name="outp", bufs=2))
         psum = ctx.enter_context(tc.psum_pool(name="psum", bufs=NPS))
         accp = ctx.enter_context(tc.psum_pool(name="accp", bufs=2))
-        if MANUAL:
-            ctx.enter_context(tc.manual_schedule())
+        ctx.enter_context(tc.manual_schedule())
 
         raw = {}
 
-        def load_h(b, kp, v0, nv):
-            t = const.tile([P, 4 * nv], BF16, name="raw", tag="raw%d_%d_%d" % (b, kp, v0))
-            view = t[:].rearrange("p (t v) -> p t v", t=4)
-            rows = h_add[b, 512 * kp : 512 * kp + 512, v0 : v0 + nv]
-            nc.sync.dma_start(out=view, in_=rows.rearrange("(p t) v -> p t v", t=4))
-            for g in range(v0 // RV, (v0 + nv) // RV):
-                raw[(b, kp, g)] = view[:, :, g * RV - v0 : g * RV - v0 + RV]
+        def load_h(b, v0, nv):
+            for kp in range(KP):
+                t = const.tile([P, 4 * nv], BF16, name="raw", tag="raw%d_%d_%d" % (b, kp, v0))
+                view = t[:].rearrange("p (t v) -> p t v", t=4)
+                rows = h_add[b, 512 * kp : 512 * kp + 512, v0 : v0 + nv]
+                nc.sync.dma_start(out=view, in_=rows.rearrange("(p t) v -> p t v", t=4))
+                for g in range(v0 // RV, (v0 + nv) // RV):
+                    raw[(b, kp, g)] = view[:, :, g * RV - v0 : g * RV - v0 + RV]
 
         hocc = {}
 
         def load_hocc(b):
-            t = const.tile([P, S], BF16, name="hocc", tag="hocc%d" % b)
-            nc.sync.dma_start(out=t[:], in_=h_occ[b])
-            hocc[b] = t
+            hocc[b] = const.tile([P, S], BF16, name="hocc", tag="hocc%d" % b)
+            nc.sync.dma_start(out=hocc[b][:], in_=h_occ[b])
+
+        w_raw = {}
+
+        def load_w(ct):
+            w_raw[ct] = const.tile([P, CMID], BF16, name="w_raw", tag="w_raw%d" % ct)
+            nc.sync.dma_start(out=w_raw[ct][:], in_=w_add2[ct * P : (ct + 1) * P, :])
 
         ones = const.tile([P, P], BF16, name="ones")
         nc.vector.memset(ones[:], 1.0)
@@ -76,33 +77,28 @@ def tile_occurrencepool_pa_t_kernel(tc, h_add, w_add2, b_add2, h_occ, w_occ3, ou
         wo_raw = const.tile([P, C8], BF16, name="wo_raw")
         nc.sync.dma_start(out=wo_raw[:], in_=w_occ3)
         nc.sync.dma_start(out=brow[0:1, :], in_=b_add2.unsqueeze(0))
-
-        w_raw = const.tile([P, NCT * CMID], BF16, name="w_raw")
-        load_h(0, 0, 0, RV)
-        load_h(0, 1, 0, RV)
-        nc.sync.dma_start(
-            out=w_raw[:].rearrange("p (a k) -> p a k", a=NCT),
-            in_=w_add2.rearrange("(a p) k -> p a k", p=P),
-        )
-        load_h(0, 0, RV, RV)
-        load_h(0, 1, RV, RV)
+        load_w(0)
+        load_h(0, 0, RV)
+        for ct in range(1, NCT):
+            load_w(ct)
+        load_h(0, RV, RV)
         load_hocc(0)
-        for g in (2, 3):
-            load_h(0, 0, g * RV, RV)
-            load_h(0, 1, g * RV, RV)
-        for h in (0, 1):
-            load_h(1, 0, h * 2 * RV, 2 * RV)
-            load_h(1, 1, h * 2 * RV, 2 * RV)
-        load_hocc(1)
-        for b in (2, 3):
-            for h in (0, 1):
-                load_h(b, 0, h * 2 * RV, 2 * RV)
-                load_h(b, 1, h * 2 * RV, 2 * RV)
+        load_h(0, 2 * RV, RV)
+        load_h(0, 3 * RV, RV)
+        for b in range(1, B):
+            load_h(b, 0, 2 * RV)
             load_hocc(b)
+            load_h(b, 2 * RV, 2 * RV)
 
         grp, hc, hs, banks, fg, fc, fs = {}, {}, {}, {}, {}, {}, {}
         og, oc, os_, acc = {}, {}, {}, {}
         emitted = set()
+
+        def first(key):
+            if key in emitted:
+                return False
+            emitted.add(key)
+            return True
 
         def segments(r, kp):
             if (r, kp) in WHOLE:
@@ -110,7 +106,7 @@ def tile_occurrencepool_pa_t_kernel(tc, h_add, w_add2, b_add2, h_occ, w_occ3, ou
             if kp == 0:
                 return [("s", 0, RV)]
             gs = GSHARE if r >= GFROM else 0
-            vs = VLATE if r >= LATE else (0 if gs else VSHARE)
+            vs = 0 if gs else VSHARE
             segs = [("s", 0, RV - vs - gs)]
             if gs:
                 segs.append(("g", RV - vs - gs, RV - vs))
@@ -122,9 +118,8 @@ def tile_occurrencepool_pa_t_kernel(tc, h_add, w_add2, b_add2, h_occ, w_occ3, ou
             b, g = divmod(r, NG)
             for kp in range(KP):
                 for eng, v0, v1 in segments(r, kp):
-                    if eng not in engines or (r, kp, v0) in emitted:
+                    if eng not in engines or not first(("r", r, kp, v0)):
                         continue
-                    emitted.add((r, kp, v0))
                     if r not in grp:
                         grp[r] = grpp.tile([P, KP * RV * 4], BF16, name="grp", align_bytes=64)
                     dst = grp[r][:].rearrange("p (k v t) -> p k v t", k=KP, v=RV, t=4)
@@ -138,20 +133,21 @@ def tile_occurrencepool_pa_t_kernel(tc, h_add, w_add2, b_add2, h_occ, w_occ3, ou
                         nc.gpsimd.tensor_scalar(out=dst, in0=src, scalar1=1.0, scalar2=0.0, op0=MULT, op1=ADD)
 
         def quantise_h(r):
-            if ("qh", r) in emitted:
+            if not first(("qh", r)):
                 return
-            emitted.add(("qh", r))
             hc[r] = hcp.tile([P, KP * RV], U32, name="hc", align_bytes=64)
             hs[r] = hcp.tile([P, KP * RV], U8, name="hs", align_bytes=64)
             nc.vector.quantize_mx(out=hc[r][:].bitcast(FP8X4), scales=hs[r][:], in_=grp[r][:])
 
         def stage1(r, ct):
+            if not first(("s1", r, ct)):
+                return
             ps = psum.tile([P, 4, P], F32, name="ps", tag="bank")
             banks[(r, ct)] = ps
             for j in range(4):
                 for kp in range(KP):
                     hcol = slice(kp * RV + j * P, kp * RV + (j + 1) * P)
-                    wcol = slice(kp * CIN + ct * P, kp * CIN + (ct + 1) * P)
+                    wcol = slice((ct * KP + kp) * P, (ct * KP + kp + 1) * P)
                     nc.tensor.matmul_mx(
                         out=ps[:, j, :],
                         lhsT=hc[r][:, hcol].bitcast(FP8X4),
@@ -182,9 +178,8 @@ def tile_occurrencepool_pa_t_kernel(tc, h_add, w_add2, b_add2, h_occ, w_occ3, ou
             )
 
         def occurrence(r):
-            if ("occ", r) in emitted:
+            if not first(("occ", r)):
                 return
-            emitted.add(("occ", r))
             b, g = divmod(r, NG)
             ps = psum.tile([P, 4, P], F32, name="ops", tag="bank")
             for j in range(4):
@@ -198,15 +193,12 @@ def tile_occurrencepool_pa_t_kernel(tc, h_add, w_add2, b_add2, h_occ, w_occ3, ou
             )
 
         def quantise_o(r):
-            if ("qo", r) in emitted:
-                return
-            emitted.add(("qo", r))
             oc[r] = op.tile([P, COUT], U32, name="oc", align_bytes=64)
             os_[r] = op.tile([P, COUT], U8, name="os", align_bytes=64)
             nc.vector.quantize_mx(out=oc[r][:].bitcast(FP8X4), scales=os_[r][:], in_=og[r][:])
 
         def halves(b):
-            if SPLIT_LAST and b == B - 1:
+            if b == B - 1:
                 return [(0, CIN // 2), (CIN // 2, CIN)]
             return [(0, CIN)]
 
@@ -246,51 +238,54 @@ def tile_occurrencepool_pa_t_kernel(tc, h_add, w_add2, b_add2, h_occ, w_occ3, ou
         bias = const.tile([P, CIN], F32, name="bias")
         nc.scalar.copy(out=bias[:], in_=b_ps[:])
 
-        regroup(0, "sv")
-        quantise_h(0)
+        wgrp = const.tile([P, NCT * KP * P * 4], BF16, name="wgrp", align_bytes=64)
+        wgf = wgrp[:].bitcast(F32).rearrange("p (a k c u) -> p a k c u", a=NCT, k=KP, c=P, u=2)
+        wc = const.tile([P, NCT * KP * P], U32, name="wc", align_bytes=64)
+        ws = const.tile([P, NCT * KP * P], U8, name="ws", align_bytes=64)
 
-        wf = w_raw[:].bitcast(F32)
-        wgrp = const.tile([P, KP * CIN * 4], BF16, name="wgrp", align_bytes=64)
-        wgf = wgrp[:].bitcast(F32).rearrange("p (k c u) -> p k c u", k=KP, c=CIN, u=2)
-        wc = const.tile([P, KP * CIN], U32, name="wc", align_bytes=64)
-        ws = const.tile([P, KP * CIN], U8, name="ws", align_bytes=64)
-        for kp in range(KP):
-            for cp in range(NCT // 2):
-                w_ps = psum.tile([P, 2, 2 * P], F32, name="w_ps", tag="bank")
+        def transpose_w(ct):
+            wf = w_raw[ct][:].bitcast(F32)
+            w_ps = psum.tile([P, 2 * KP, P], F32, name="w_ps", tag="bank")
+            for kp in range(KP):
                 for u in range(2):
-                    for h in range(2):
-                        w0 = (2 * cp + h) * 512 + 256 * kp
-                        nc.tensor.transpose(
-                            out=w_ps[:, u, h * P : (h + 1) * P],
-                            in_=wf[:, w0 + u : w0 + 256 : 2],
-                            identity=ident_f[:],
-                        )
-                nc.scalar.copy(
-                    out=wgf[:, kp, 2 * cp * P : (2 * cp + 2) * P, :],
-                    in_=w_ps[:].rearrange("p u c -> p c u"),
-                )
-        regroup(1, "sv")
-        for kp in range(KP):
+                    nc.tensor.transpose(
+                        out=w_ps[:, 2 * kp + u, :],
+                        in_=wf[:, 256 * kp + u : 256 * kp + 256 : 2],
+                        identity=ident_f[:],
+                    )
+            nc.scalar.copy(out=wgf[:, ct], in_=w_ps[:].rearrange("p (k u) c -> p k c u", u=2))
+
+        def quantise_w(ct):
+            n = KP * P
             nc.vector.quantize_mx(
-                out=wc[:, kp * CIN : (kp + 1) * CIN].bitcast(FP8X4),
-                scales=ws[:, kp * CIN : (kp + 1) * CIN],
-                in_=wgrp[:, kp * CIN * 4 : (kp + 1) * CIN * 4],
+                out=wc[:, ct * n : (ct + 1) * n].bitcast(FP8X4),
+                scales=ws[:, ct * n : (ct + 1) * n],
+                in_=wgrp[:, ct * n * 4 : (ct + 1) * n * 4],
             )
+
+        transpose_w(0)
+        regroup(0, "sv")
+        quantise_w(0)
+        quantise_h(0)
+        for ct in range(1, NCT):
+            transpose_w(ct)
+        for ct in range(1, NCT):
+            quantise_w(ct)
+        for ct in range(NCT):
+            stage1(0, ct)
+        regroup(1, "sv")
         quantise_h(1)
-        occurrence(0)
-        occurrence(1)
-        quantise_o(0)
 
         def live(r):
             return 0 <= r < NR
 
         last = NR - 1
-        for i in range(-LS, NR + 1):
+        for i in range(-LS, NR):
             if live(i + LS):
                 regroup(i + LS, "sg")
             if live(i + 1):
                 stage1(i + 1, 0)
-            if live(i - 1) and not (SPLIT_LAST and i - 1 == last):
+            if live(i - 1):
                 for c0, c1 in halves((i - 1) // NG):
                     stage2(i - 1, c0, c1)
             for ct in range(NCT):
@@ -298,7 +293,9 @@ def tile_occurrencepool_pa_t_kernel(tc, h_add, w_add2, b_add2, h_occ, w_occ3, ou
                     evacuate(i, ct)
                 if ct + 1 < NCT and live(i + 1):
                     stage1(i + 1, ct + 1)
-                if SPLIT_LAST and i == last and ct % 2 == 1:
+                if i == last and ct == 0:
+                    quantise_o(i)
+                if i == last and ct % 2 == 1:
                     c0, c1 = halves(B - 1)[ct // 2]
                     quantise_f(i, c0, c1)
                     stage2(i, c0, c1)
@@ -308,11 +305,11 @@ def tile_occurrencepool_pa_t_kernel(tc, h_add, w_add2, b_add2, h_occ, w_occ3, ou
             for q in QORDER:
                 if q == "H" and live(i + 2):
                     quantise_h(i + 2)
-                if q == "O" and live(i + 1):
-                    quantise_o(i + 1)
-                if q == "F" and live(i) and not (SPLIT_LAST and i == last):
+                if q == "O" and live(i) and i != last:
+                    quantise_o(i)
+                if q == "F" and live(i) and i != last:
                     quantise_f(i, 0, CIN)
             if live(i + LV):
                 regroup(i + LV, "v")
-            if i >= NG and i % NG == 0 and not (SPLIT_LAST and i == NR):
+            if i >= NG and i % NG == 0:
                 finish(i // NG - 1, 0, CIN)

@@ -45,7 +45,6 @@ def tile_occurrencepool_pa_t_kernel(tc, h_add, w_add2, b_add2, h_occ, w_occ3, ou
         outp = ctx.enter_context(tc.tile_pool(name="outp", bufs=2))
         psum = ctx.enter_context(tc.psum_pool(name="psum", bufs=NPS))
         accp = ctx.enter_context(tc.psum_pool(name="accp", bufs=2))
-        ctx.enter_context(tc.manual_schedule())
 
         raw = {}
 

@@ -26,7 +26,7 @@ LS = 4
 LV = 3
 LO = 2
 VSHARE = 128
-WHOLE = {(0, 0): "v", (0, 1): "v", (1, 0): "s", (1, 1): "v"}
+WHOLE = {(0, 0): "v", (0, 1): "v", (1, 0): "v", (1, 1): "v"}
 GSHARE = 192
 GFROM = 2
 QORDER = "OFH"

@@ -27,8 +27,9 @@ LV = 3
 LO = 2
 VSHARE = 128
 WHOLE = {(0, 0): "v", (0, 1): "v", (1, 0): "v", (1, 1): "v"}
-GSHARE = 192
+GSHARE = 256
 GFROM = 2
+SWAPR = 3
 QORDER = "OFH"
 NBG = 3
 NPS = 6
@@ -41,6 +42,7 @@ def tile_occurrencepool_pa_t_kernel(tc, h_add, w_add2, b_add2, h_occ, w_occ3, ou
         grpp = ctx.enter_context(tc.tile_pool(name="grpp", bufs=NBG))
         hcp = ctx.enter_context(tc.tile_pool(name="hcp", bufs=2))
         fp = ctx.enter_context(tc.tile_pool(name="fp", bufs=2))
+        ftp = ctx.enter_context(tc.tile_pool(name="ftp", bufs=4))
         op = ctx.enter_context(tc.tile_pool(name="op", bufs=3))
         outp = ctx.enter_context(tc.tile_pool(name="outp", bufs=2))
         psum = ctx.enter_context(tc.psum_pool(name="psum", bufs=NPS))
@@ -74,10 +76,10 @@ def tile_occurrencepool_pa_t_kernel(tc, h_add, w_add2, b_add2, h_occ, w_occ3, ou
         brow = const.tile([P, CIN], BF16, name="brow")
         nc.vector.memset(brow[:], 0.0)
         wo_raw = const.tile([P, C8], BF16, name="wo_raw")
+        load_h(0, 0, RV)
+        load_w(0)
         nc.sync.dma_start(out=wo_raw[:], in_=w_occ3)
         nc.sync.dma_start(out=brow[0:1, :], in_=b_add2.unsqueeze(0))
-        load_w(0)
-        load_h(0, 0, RV)
         for ct in range(1, NCT):
             load_w(ct)
         load_h(0, RV, RV)
@@ -122,8 +124,13 @@ def tile_occurrencepool_pa_t_kernel(tc, h_add, w_add2, b_add2, h_occ, w_occ3, ou
                     if r not in grp:
                         grp[r] = grpp.tile([P, KP * RV * 4], BF16, name="grp", align_bytes=64)
                     dst = grp[r][:].rearrange("p (k v t) -> p k v t", k=KP, v=RV, t=4)
-                    dst = dst[:, kp, v0:v1, :].rearrange("p (c i) t -> p c t i", i=4)
-                    src = raw[(b, kp, g)][:, :, v0:v1].rearrange("p t (c i) -> p c t i", i=4)
+                    dst = dst[:, kp, v0:v1, :]
+                    src = raw[(b, kp, g)][:, :, v0:v1]
+                    if eng == "g":
+                        src = src.rearrange("p t v -> p v t")
+                    else:
+                        dst = dst.rearrange("p (c i) t -> p c t i", i=4)
+                        src = src.rearrange("p t (c i) -> p c t i", i=4)
                     if eng == "v":
                         nc.vector.tensor_copy(out=dst, in_=src)
                     elif eng == "s":
@@ -138,8 +145,54 @@ def tile_occurrencepool_pa_t_kernel(tc, h_add, w_add2, b_add2, h_occ, w_occ3, ou
             hs[r] = hcp.tile([P, KP * RV], U8, name="hs", align_bytes=64)
             nc.vector.quantize_mx(out=hc[r][:].bitcast(FP8X4), scales=hs[r][:], in_=grp[r][:])
 
+        def swapped(r, ct):
+            return ct >= NCT - 2 and r >= NR - SWAPR
+
+        ft, flipped = {}, {}
+
+        def stage1_swapped(r, ct):
+            ps = psum.tile([P, RV], F32, name="sw_ps", tag="bank")
+            for kp in range(KP):
+                wcol = slice((ct * KP + kp) * P, (ct * KP + kp + 1) * P)
+                hcol = slice(kp * RV, (kp + 1) * RV)
+                nc.tensor.matmul_mx(
+                    out=ps[:],
+                    lhsT=wc[:, wcol].bitcast(FP8X4),
+                    lhsT_scale=ws[:, wcol],
+                    rhs=hc[r][:, hcol].bitcast(FP8X4),
+                    rhs_scale=hs[r][:, hcol],
+                    start=(kp == 0),
+                    stop=(kp == KP - 1),
+                )
+            ft[(r, ct)] = ftp.tile([P, RV], BF16, name="ft", align_bytes=64)
+            nc.scalar.activation(
+                out=ft[(r, ct)][:].rearrange("c (u p e) -> c u p e", u=2, p=P),
+                in_=ps[:].rearrange("c (u e p) -> c u p e", u=2, e=2),
+                func=ACT.Identity,
+                bias=bcol[:, ct : ct + 1],
+            )
+
+        def flip(r, ct):
+            words = ft[(r, ct)][:].bitcast(F32)
+            ps = psum.tile([P, 2, P], F32, name="fl_ps", tag="bank")
+            for u in range(2):
+                nc.tensor.transpose(out=ps[:, u, :], in_=words[:, u * P : (u + 1) * P], identity=ident_f[:])
+            flipped[(r, ct)] = ps
+
+        def feat_tile(r):
+            if r not in fg:
+                fg[r] = fp.tile([P, CIN * 4], BF16, name="fg", align_bytes=64)
+
+        def unflip(r, ct):
+            feat_tile(r)
+            dst = fg[r][:].bitcast(F32).rearrange("p (c u) -> p c u", u=2)[:, ct * P : (ct + 1) * P, :]
+            nc.scalar.copy(out=dst, in_=flipped[(r, ct)][:].rearrange("p u c -> p c u"))
+
         def stage1(r, ct):
             if not first(("s1", r, ct)):
+                return
+            if swapped(r, ct):
+                stage1_swapped(r, ct)
                 return
             ps = psum.tile([P, 4, P], F32, name="ps", tag="bank")
             banks[(r, ct)] = ps
@@ -158,8 +211,9 @@ def tile_occurrencepool_pa_t_kernel(tc, h_add, w_add2, b_add2, h_occ, w_occ3, ou
                     )
 
         def evacuate(r, ct):
-            if ct == 0:
-                fg[r] = fp.tile([P, CIN * 4], BF16, name="fg", align_bytes=64)
+            if swapped(r, ct):
+                return
+            feat_tile(r)
             dst = fg[r][:].rearrange("p (c j) -> p c j", j=4)[:, ct * P : (ct + 1) * P, :]
             nc.vector.tensor_tensor(
                 out=dst,
@@ -237,6 +291,18 @@ def tile_occurrencepool_pa_t_kernel(tc, h_add, w_add2, b_add2, h_occ, w_occ3, ou
         bias = const.tile([P, CIN], F32, name="bias")
         nc.scalar.copy(out=bias[:], in_=b_ps[:])
 
+        bc_ps = psum.tile([P, NCT], F32, name="bc_ps", tag="bank")
+        for ct in range(NCT):
+            nc.tensor.matmul(
+                out=bc_ps[:, ct : ct + 1],
+                lhsT=brow[:, ct * P : (ct + 1) * P],
+                rhs=ones[:, 0:1],
+                start=True,
+                stop=True,
+            )
+        bcol = const.tile([P, NCT], F32, name="bcol")
+        nc.scalar.copy(out=bcol[:], in_=bc_ps[:])
+
         wgrp = const.tile([P, NCT * KP * P * 4], BF16, name="wgrp", align_bytes=64)
         wgf = wgrp[:].bitcast(F32).rearrange("p (a k c u) -> p a k c u", a=NCT, k=KP, c=P, u=2)
         wc = const.tile([P, NCT * KP * P], U32, name="wc", align_bytes=64)
@@ -280,8 +346,15 @@ def tile_occurrencepool_pa_t_kernel(tc, h_add, w_add2, b_add2, h_occ, w_occ3, ou
 
         last = NR - 1
         for i in range(-LS, NR):
+            for ct in range(NCT):
+                if live(i) and swapped(i, ct):
+                    flip(i, ct)
+                    unflip(i, ct)
             if live(i + LS):
                 regroup(i + LS, "sg")
+            for ct in range(NCT):
+                if live(i + 1) and swapped(i + 1, ct):
+                    stage1(i + 1, ct)
             if live(i + 1):
                 stage1(i + 1, 0)
             if live(i - 1):

@@ -83,8 +83,8 @@ def tile_occurrencepool_pa_t_kernel(tc, h_add, w_add2, b_add2, h_occ, w_occ3, ou
         for ct in range(1, NCT):
             load_w(ct)
         load_h(0, RV, RV)
-        load_hocc(0)
         load_h(0, 2 * RV, RV)
+        load_hocc(0)
         load_h(0, 3 * RV, RV)
         for b in range(1, B):
             load_h(b, 0, 2 * RV)
@@ -129,8 +129,9 @@ def tile_occurrencepool_pa_t_kernel(tc, h_add, w_add2, b_add2, h_occ, w_occ3, ou
                     if eng == "g":
                         src = src.rearrange("p t v -> p v t")
                     else:
-                        dst = dst.rearrange("p (c i) t -> p c t i", i=4)
-                        src = src.rearrange("p t (c i) -> p c t i", i=4)
+                        run = 8 if eng == "s" else 4
+                        dst = dst.rearrange("p (c i) t -> p c t i", i=run)
+                        src = src.rearrange("p t (c i) -> p c t i", i=run)
                     if eng == "v":
                         nc.vector.tensor_copy(out=dst, in_=src)
                     elif eng == "s":

from contextlib import ExitStack

import concourse.mybir as mybir
from concourse.masks import make_identity

F32 = mybir.dt.float32
BF16 = mybir.dt.bfloat16
U32 = mybir.dt.uint32
U8 = mybir.dt.uint8
FP8X4 = mybir.dt.float8_e4m3fn_x4
ADD = mybir.AluOpType.add
MULT = mybir.AluOpType.mult
ACT = mybir.ActivationFunctionType

P = 128
B, CIN, CMID, C8, COUT, S = 4, 512, 1024, 128, 128, 2048
KP = CMID // 512
RV = 512
NG = S // RV
NR = B * NG
NCT = CIN // P

FLOPS = 2 * B * S * (CIN * CMID + COUT * C8 + COUT * CIN)

LS = 4
LV = 3
LO = 2
VSHARE = 128
WHOLE = {(0, 0): "v", (0, 1): "v", (1, 0): "v", (1, 1): "v"}
GSHARE = 256
GFROM = 2
SWAPR = 3
QORDER = "OFH"
NBG = 3
NPS = 6


def tile_occurrencepool_pa_t_kernel(tc, h_add, w_add2, b_add2, h_occ, w_occ3, out):
    nc = tc.nc
    with ExitStack() as ctx:
        const = ctx.enter_context(tc.tile_pool(name="const", bufs=1))
        grpp = ctx.enter_context(tc.tile_pool(name="grpp", bufs=NBG))
        hcp = ctx.enter_context(tc.tile_pool(name="hcp", bufs=2))
        fp = ctx.enter_context(tc.tile_pool(name="fp", bufs=2))
        ftp = ctx.enter_context(tc.tile_pool(name="ftp", bufs=4))
        op = ctx.enter_context(tc.tile_pool(name="op", bufs=3))
        outp = ctx.enter_context(tc.tile_pool(name="outp", bufs=2))
        psum = ctx.enter_context(tc.psum_pool(name="psum", bufs=NPS))
        accp = ctx.enter_context(tc.psum_pool(name="accp", bufs=2))

        raw = {}

        def load_h(b, v0, nv):
            for kp in range(KP):
                t = const.tile([P, 4 * nv], BF16, name="raw", tag="raw%d_%d_%d" % (b, kp, v0))
                view = t[:].rearrange("p (t v) -> p t v", t=4)
                rows = h_add[b, 512 * kp : 512 * kp + 512, v0 : v0 + nv]
                nc.sync.dma_start(out=view, in_=rows.rearrange("(p t) v -> p t v", t=4))
                for g in range(v0 // RV, (v0 + nv) // RV):
                    raw[(b, kp, g)] = view[:, :, g * RV - v0 : g * RV - v0 + RV]

        hocc = {}

        def load_hocc(b):
            hocc[b] = const.tile([P, S], BF16, name="hocc", tag="hocc%d" % b)
            nc.sync.dma_start(out=hocc[b][:], in_=h_occ[b])

        w_raw = {}

        def load_w(ct):
            w_raw[ct] = const.tile([P, CMID], BF16, name="w_raw", tag="w_raw%d" % ct)
            nc.sync.dma_start(out=w_raw[ct][:], in_=w_add2[ct * P : (ct + 1) * P, :])

        ones = const.tile([P, P], BF16, name="ones")
        nc.vector.memset(ones[:], 1.0)
        brow = const.tile([P, CIN], BF16, name="brow")
        nc.vector.memset(brow[:], 0.0)
        wo_raw = const.tile([P, C8], BF16, name="wo_raw")
        load_h(0, 0, RV)
        load_w(0)
        nc.sync.dma_start(out=wo_raw[:], in_=w_occ3)
        nc.sync.dma_start(out=brow[0:1, :], in_=b_add2.unsqueeze(0))
        for ct in range(1, NCT):
            load_w(ct)
        load_h(0, RV, RV)
        load_h(0, 2 * RV, RV)
        load_hocc(0)
        load_h(0, 3 * RV, RV)
        for b in range(1, B):
            load_h(b, 0, 2 * RV)
            load_hocc(b)
            load_h(b, 2 * RV, 2 * RV)

        grp, hc, hs, banks, fg, fc, fs = {}, {}, {}, {}, {}, {}, {}
        og, oc, os_, acc = {}, {}, {}, {}
        emitted = set()

        def first(key):
            if key in emitted:
                return False
            emitted.add(key)
            return True

        def segments(r, kp):
            if (r, kp) in WHOLE:
                return [(WHOLE[(r, kp)], 0, RV)]
            if kp == 0:
                return [("s", 0, RV)]
            gs = GSHARE if r >= GFROM else 0
            vs = 0 if gs else VSHARE
            segs = [("s", 0, RV - vs - gs)]
            if gs:
                segs.append(("g", RV - vs - gs, RV - vs))
            if vs:
                segs.append(("v", RV - vs, RV))
            return segs

        def regroup(r, engines):
            b, g = divmod(r, NG)
            for kp in range(KP):
                for eng, v0, v1 in segments(r, kp):
                    if eng not in engines or not first(("r", r, kp, v0)):
                        continue
                    if r not in grp:
                        grp[r] = grpp.tile([P, KP * RV * 4], BF16, name="grp", align_bytes=64)
                    dst = grp[r][:].rearrange("p (k v t) -> p k v t", k=KP, v=RV, t=4)
                    dst = dst[:, kp, v0:v1, :]
                    src = raw[(b, kp, g)][:, :, v0:v1]
                    if eng == "g":
                        src = src.rearrange("p t v -> p v t")
                    else:
                        run = 8 if eng == "s" else 4
                        dst = dst.rearrange("p (c i) t -> p c t i", i=run)
                        src = src.rearrange("p t (c i) -> p c t i", i=run)
                    if eng == "v":
                        nc.vector.tensor_copy(out=dst, in_=src)
                    elif eng == "s":
                        nc.scalar.copy(out=dst, in_=src)
                    else:
                        nc.gpsimd.tensor_scalar(out=dst, in0=src, scalar1=1.0, scalar2=0.0, op0=MULT, op1=ADD)

        def quantise_h(r):
            if not first(("qh", r)):
                return
            hc[r] = hcp.tile([P, KP * RV], U32, name="hc", align_bytes=64)
            hs[r] = hcp.tile([P, KP * RV], U8, name="hs", align_bytes=64)
            nc.vector.quantize_mx(out=hc[r][:].bitcast(FP8X4), scales=hs[r][:], in_=grp[r][:])

        def swapped(r, ct):
            return ct >= NCT - 2 and r >= NR - SWAPR

        ft, flipped = {}, {}

        def stage1_swapped(r, ct):
            ps = psum.tile([P, RV], F32, name="sw_ps", tag="bank")
            for kp in range(KP):
                wcol = slice((ct * KP + kp) * P, (ct * KP + kp + 1) * P)
                hcol = slice(kp * RV, (kp + 1) * RV)
                nc.tensor.matmul_mx(
                    out=ps[:],
                    lhsT=wc[:, wcol].bitcast(FP8X4),
                    lhsT_scale=ws[:, wcol],
                    rhs=hc[r][:, hcol].bitcast(FP8X4),
                    rhs_scale=hs[r][:, hcol],
                    start=(kp == 0),
                    stop=(kp == KP - 1),
                )
            ft[(r, ct)] = ftp.tile([P, RV], BF16, name="ft", align_bytes=64)
            nc.scalar.activation(
                out=ft[(r, ct)][:].rearrange("c (u p e) -> c u p e", u=2, p=P),
                in_=ps[:].rearrange("c (u e p) -> c u p e", u=2, e=2),
                func=ACT.Identity,
                bias=bcol[:, ct : ct + 1],
            )

        def flip(r, ct):
            words = ft[(r, ct)][:].bitcast(F32)
            ps = psum.tile([P, 2, P], F32, name="fl_ps", tag="bank")
            for u in range(2):
                nc.tensor.transpose(out=ps[:, u, :], in_=words[:, u * P : (u + 1) * P], identity=ident_f[:])
            flipped[(r, ct)] = ps

        def feat_tile(r):
            if r not in fg:
                fg[r] = fp.tile([P, CIN * 4], BF16, name="fg", align_bytes=64)

        def unflip(r, ct):
            feat_tile(r)
            dst = fg[r][:].bitcast(F32).rearrange("p (c u) -> p c u", u=2)[:, ct * P : (ct + 1) * P, :]
            nc.scalar.copy(out=dst, in_=flipped[(r, ct)][:].rearrange("p u c -> p c u"))

        def stage1(r, ct):
            if not first(("s1", r, ct)):
                return
            if swapped(r, ct):
                stage1_swapped(r, ct)
                return
            ps = psum.tile([P, 4, P], F32, name="ps", tag="bank")
            banks[(r, ct)] = ps
            for j in range(4):
                for kp in range(KP):
                    hcol = slice(kp * RV + j * P, kp * RV + (j + 1) * P)
                    wcol = slice((ct * KP + kp) * P, (ct * KP + kp + 1) * P)
                    nc.tensor.matmul_mx(
                        out=ps[:, j, :],
                        lhsT=hc[r][:, hcol].bitcast(FP8X4),
                        lhsT_scale=hs[r][:, hcol],
                        rhs=wc[:, wcol].bitcast(FP8X4),
                        rhs_scale=ws[:, wcol],
                        start=(kp == 0),
                        stop=(kp == KP - 1),
                    )

        def evacuate(r, ct):
            if swapped(r, ct):
                return
            feat_tile(r)
            dst = fg[r][:].rearrange("p (c j) -> p c j", j=4)[:, ct * P : (ct + 1) * P, :]
            nc.vector.tensor_tensor(
                out=dst,
                in0=banks[(r, ct)][:].rearrange("p j c -> p c j"),
                in1=bias[:, ct * P : (ct + 1) * P].unsqueeze(2).to_broadcast([P, P, 4]),
                op=ADD,
            )

        def quantise_f(r, c0, c1):
            if c0 == 0:
                fc[r] = fp.tile([P, CIN], U32, name="fc", align_bytes=64)
                fs[r] = fp.tile([P, CIN], U8, name="fs", align_bytes=64)
            nc.vector.quantize_mx(
                out=fc[r][:, c0:c1].bitcast(FP8X4), scales=fs[r][:, c0:c1], in_=fg[r][:, 4 * c0 : 4 * c1]
            )

        def occurrence(r):
            if not first(("occ", r)):
                return
            b, g = divmod(r, NG)
            ps = psum.tile([P, 4, P], F32, name="ops", tag="bank")
            for j in range(4):
                v0 = g * RV + j * P
                nc.tensor.matmul(out=ps[:, j, :], lhsT=hocc[b][:, v0 : v0 + P], rhs=woT[:], start=True, stop=True)
            og[r] = op.tile([P, COUT * 4], BF16, name="og", align_bytes=64)
            nc.scalar.activation(
                out=og[r][:].rearrange("p (o j) -> p o j", j=4),
                in_=ps[:].rearrange("p j o -> p o j"),
                func=ACT.Abs,
            )

        def quantise_o(r):
            oc[r] = op.tile([P, COUT], U32, name="oc", align_bytes=64)
            os_[r] = op.tile([P, COUT], U8, name="os", align_bytes=64)
            nc.vector.quantize_mx(out=oc[r][:].bitcast(FP8X4), scales=os_[r][:], in_=og[r][:])

        def halves(b):
            if b == B - 1:
                return [(0, CIN // 2), (CIN // 2, CIN)]
            return [(0, CIN)]

        def stage2(r, c0, c1):
            b, g = divmod(r, NG)
            if g == 0:
                acc[(b, c0)] = accp.tile([P, c1 - c0], F32, name="acc")
            nc.tensor.matmul_mx(
                out=acc[(b, c0)][:],
                lhsT=oc[r][:].bitcast(FP8X4),
                lhsT_scale=os_[r][:],
                rhs=fc[r][:, c0:c1].bitcast(FP8X4),
                rhs_scale=fs[r][:, c0:c1],
                start=(g == 0),
                stop=(g == NG - 1),
            )

        def finish(b, c0, c1):
            ob = outp.tile([P, c1 - c0], F32, name="ob")
            nc.scalar.mul(out=ob[:], in_=acc[(b, c0)][:], mul=1.0 / S)
            nc.sync.dma_start(out=out[b, :, c0:c1], in_=ob[:])

        ident_f = const.tile([P, P], F32, name="ident_f")
        make_identity(nc, ident_f[:])
        ident_b = const.tile([P, P], BF16, name="ident_b")
        make_identity(nc, ident_b[:])
        scr = const.tile([P, 1], F32, name="scr")
        nc.scalar.activation(out=scr[:], in_=ones[:, 0:1], func=ACT.Abs)

        wo_ps = psum.tile([P, P], BF16, name="wo_ps", tag="bank")
        nc.tensor.transpose(out=wo_ps[:], in_=wo_raw[:], identity=ident_b[:])
        woT = const.tile([P, COUT], BF16, name="woT")
        nc.scalar.copy(out=woT[:], in_=wo_ps[:])

        b_ps = psum.tile([P, CIN], F32, name="b_ps", tag="bank")
        nc.tensor.matmul(out=b_ps[:], lhsT=ones[:], rhs=brow[:], start=True, stop=True)
        bias = const.tile([P, CIN], F32, name="bias")
        nc.scalar.copy(out=bias[:], in_=b_ps[:])

        bc_ps = psum.tile([P, NCT], F32, name="bc_ps", tag="bank")
        for ct in range(NCT):
            nc.tensor.matmul(
                out=bc_ps[:, ct : ct + 1],
                lhsT=brow[:, ct * P : (ct + 1) * P],
                rhs=ones[:, 0:1],
                start=True,
                stop=True,
            )
        bcol = const.tile([P, NCT], F32, name="bcol")
        nc.scalar.copy(out=bcol[:], in_=bc_ps[:])

        wgrp = const.tile([P, NCT * KP * P * 4], BF16, name="wgrp", align_bytes=64)
        wgf = wgrp[:].bitcast(F32).rearrange("p (a k c u) -> p a k c u", a=NCT, k=KP, c=P, u=2)
        wc = const.tile([P, NCT * KP * P], U32, name="wc", align_bytes=64)
        ws = const.tile([P, NCT * KP * P], U8, name="ws", align_bytes=64)

        def transpose_w(ct):
            wf = w_raw[ct][:].bitcast(F32)
            w_ps = psum.tile([P, 2 * KP, P], F32, name="w_ps", tag="bank")
            for kp in range(KP):
                for u in range(2):
                    nc.tensor.transpose(
                        out=w_ps[:, 2 * kp + u, :],
                        in_=wf[:, 256 * kp + u : 256 * kp + 256 : 2],
                        identity=ident_f[:],
                    )
            nc.scalar.copy(out=wgf[:, ct], in_=w_ps[:].rearrange("p (k u) c -> p k c u", u=2))

        def quantise_w(ct):
            n = KP * P
            nc.vector.quantize_mx(
                out=wc[:, ct * n : (ct + 1) * n].bitcast(FP8X4),
                scales=ws[:, ct * n : (ct + 1) * n],
                in_=wgrp[:, ct * n * 4 : (ct + 1) * n * 4],
            )

        transpose_w(0)
        regroup(0, "sv")
        quantise_w(0)
        quantise_h(0)
        for ct in range(1, NCT):
            transpose_w(ct)
        for ct in range(1, NCT):
            quantise_w(ct)
        for ct in range(NCT):
            stage1(0, ct)
        regroup(1, "sv")
        quantise_h(1)

        def live(r):
            return 0 <= r < NR

        last = NR - 1
        for i in range(-LS, NR):
            for ct in range(NCT):
                if live(i) and swapped(i, ct):
                    flip(i, ct)
                    unflip(i, ct)
            if live(i + LS):
                regroup(i + LS, "sg")
            for ct in range(NCT):
                if live(i + 1) and swapped(i + 1, ct):
                    stage1(i + 1, ct)
            if live(i + 1):
                stage1(i + 1, 0)
            if live(i - 1):
                for c0, c1 in halves((i - 1) // NG):
                    stage2(i - 1, c0, c1)
            for ct in range(NCT):
                if live(i):
                    evacuate(i, ct)
                if ct + 1 < NCT and live(i + 1):
                    stage1(i + 1, ct + 1)
                if i == last and ct == 0:
                    quantise_o(i)
                if i == last and ct % 2 == 1:
                    c0, c1 = halves(B - 1)[ct // 2]
                    quantise_f(i, c0, c1)
                    stage2(i, c0, c1)
                    finish(B - 1, c0, c1)
            if live(i + LO):
                occurrence(i + LO)
            for q in QORDER:
                if q == "H" and live(i + 2):
                    quantise_h(i + 2)
                if q == "O" and live(i) and i != last:
                    quantise_o(i)
                if q == "F" and live(i) and i != last:
                    quantise_f(i, 0, CIN)
            if live(i + LV):
                regroup(i + LV, "v")
            if i >= NG and i % NG == 0:
                finish(i // NG - 1, 0, CIN)
